import numpy as np
import ml_dtypes


def mxq(x, axis, fmt="e4m3"):
    dtype, down = {"e4m3": (ml_dtypes.float8_e4m3fn, 7), "e5m2": (ml_dtypes.float8_e5m2, 14)}[fmt]
    v = np.moveaxis(np.asarray(x, np.float32).astype(ml_dtypes.bfloat16).astype(np.float64), axis, -1)
    blocks = v.reshape(v.shape[:-1] + (-1, 32))
    amax = np.abs(blocks).max(-1, keepdims=True)
    byte = np.maximum(np.where(amax > 0, np.frexp(amax)[1] - 1 + 127, 0) - down, 1)
    scale = np.exp2(byte - 127.0)
    codes = (blocks / scale).astype(np.float32).astype(dtype).astype(np.float64)
    return np.moveaxis((codes * scale).reshape(v.shape), -1, axis)


WIDE = False


def mx_kscale(k):
    if not WIDE:
        return np.ones(k)
    levels = np.array([10, -10, 5, -5, 0])
    a = np.random.permutation(np.resize(levels, k // 512 * 4)).reshape(k // 512, 4)
    idx = np.arange(k)
    return np.exp2(a[idx // 512, idx % 128 // 32])


BF16 = ml_dtypes.bfloat16


def bf(x):
    return np.asarray(x, np.float32).astype(BF16)


def f64(x):
    return np.asarray(x).astype(np.float64)


B, SD, A, H, HS, M, C, F1, F2 = 4096, 896, 128, 512, 32, 896, 2, 2048, 300
K1 = SD + A
EPS = 1e-12


def l2norm(v):
    n = np.sqrt(np.sum(v * v, axis=-1, keepdims=True))
    return v / np.maximum(n, EPS)


def setup_inputs():
    s = mx_kscale(K1)
    g = np.where(np.arange(H) < HS, 1.0, 0.125)
    return {"state": bf(np.random.standard_normal((B, SD)) * s[:SD]),
            "action": bf(np.random.standard_normal((B, A)) * s[SD:]),
            "up_w1": bf(np.random.standard_normal((H, K1)) * g[:, None] / np.sqrt(K1) / s[None, :]),
            "up_b1": bf(np.random.standard_normal(H) * 0.5 * g),
            "up_w2_self": bf(np.random.standard_normal((H, H))),
            "up_b2": bf(np.random.standard_normal(H) * 0.3)}


def reference(state, action, up_w1, up_b1, up_w2_self, up_b2):
    xu = np.concatenate([f64(state), f64(action)], axis=-1)
    z = (mxq(xu, 1, "e4m3") @ mxq(f64(up_w1), 1, "e4m3").T) + f64(up_b1)
    t = np.tanh(l2norm(z))
    return np.tanh((mxq(t, 1, "e4m3") @ mxq(f64(up_w2_self), 1, "e4m3").T) + f64(up_b2))

@@ -1,0 +1,309 @@
+from contextlib import ExitStack
+
+import concourse.mybir as mybir
+from concourse.masks import make_identity
+
+F32 = mybir.dt.float32
+BF16 = mybir.dt.bfloat16
+U32 = mybir.dt.uint32
+U8 = mybir.dt.uint8
+FP8X4 = mybir.dt.float8_e4m3fn_x4
+ACT = mybir.ActivationFunctionType
+ALU = mybir.AluOpType
+
+P = 128
+PACK = 4
+K_PASS = P * PACK
+BATCH, STATE, ACTION, HIDDEN = 4096, 896, 128, 512
+K1 = STATE + ACTION
+PASSES_1 = K1 // K_PASS
+TILES = BATCH // P
+CHUNK = 2
+EPS = 1e-12
+BANK_WORDS = 512
+
+FLOPS = 2 * BATCH * K1 * HIDDEN + 2 * BATCH * HIDDEN * HIDDEN
+
+LAG_COPY_X = 1
+LAG_MATMUL_1 = 2
+LAG_BIAS_1 = 3
+LAG_SCALE = 4
+LAG_TRANSPOSE_Z = 5
+LAG_TANH_1 = 6
+LAG_MATMUL_2 = 7
+LAG_OUT = 8
+STEPS = TILES + LAG_OUT
+
+
+def tile_modelgraphpolicy_pa_t_kernel(
+    tc, state, action, up_w1, up_b1, up_w2_self, up_b2, out
+):
+    nc = tc.nc
+    state_rows = state.rearrange("(p t) d -> p t d", t=TILES)
+    action_rows = action.rearrange("(p t) d -> p t d", t=TILES)
+    out_rows = out.rearrange("(p t) d -> p t d", t=TILES)
+
+    with ExitStack() as stack:
+        const = stack.enter_context(tc.tile_pool(name="const", bufs=1))
+        work = stack.enter_context(tc.tile_pool(name="work", bufs=4))
+        psum = stack.enter_context(tc.psum_pool(name="psum", bufs=2))
+        stack.enter_context(tc.manual_schedule())
+
+        bias_rows = const.tile([P, 2 * HIDDEN], BF16)
+        nc.vector.memset(bias_rows[:], 0.0)
+        nc.scalar.dma_start(
+            out=bias_rows[0:1, 0:HIDDEN], in_=up_b1.rearrange("(o h) -> o h", o=1)
+        )
+        nc.scalar.dma_start(
+            out=bias_rows[0:1, HIDDEN : 2 * HIDDEN], in_=up_b2.rearrange("(o h) -> o h", o=1)
+        )
+
+        w1_rows = const.tile([P, PACK, K1], BF16)
+        nc.sync.dma_start(out=w1_rows[:], in_=up_w1.rearrange("(p j) k -> p j k", j=PACK))
+        w2_rows = const.tile([P, PACK, HIDDEN], BF16)
+
+        x_chunks = []
+
+        def load_x(c):
+            x = const.tile([P, CHUNK, K1], BF16, name="x%d" % c)
+            tiles = slice(c * CHUNK, (c + 1) * CHUNK)
+            nc.sync.dma_start(out=x[:, :, 0:STATE], in_=state_rows[:, tiles, :])
+            nc.sync.dma_start(out=x[:, :, STATE:K1], in_=action_rows[:, tiles, :])
+            x_chunks.append(x)
+
+        load_x(0)
+        nc.sync.dma_start(out=w2_rows[:], in_=up_w2_self.rearrange("(c p) k -> p c k", p=P))
+        for c in range(1, TILES // CHUNK):
+            load_x(c)
+
+        zero_col = const.tile([P, 1], F32)
+        nc.vector.memset(zero_col[:], 0.0)
+        table_warm = const.tile([P, 1], F32)
+        nc.scalar.activation(out=table_warm[:], in_=zero_col[:], func=ACT.Tanh)
+
+        ones = const.tile([P, P], BF16)
+        nc.vector.memset(ones[:], 1.0)
+        minus_half = const.tile([P, 1], F32)
+        nc.vector.memset(minus_half[:], -0.5)
+        ident = const.tile([P, P], F32)
+        make_identity(nc, ident[:])
+
+        def interleave_out_of_psum(copy, grouped, bank):
+            copy(
+                out=grouped.bitcast(F32).rearrange("q (a n u) -> q a n u", a=2, u=2),
+                in_=bank[:].rearrange("q (a u) n -> q a n u", u=2),
+            )
+
+        b1_bank = psum.tile([P, HIDDEN], F32, tag="a")
+        nc.tensor.matmul(
+            out=b1_bank[:], lhsT=ones[:], rhs=bias_rows[:, 0:HIDDEN], start=True, stop=True
+        )
+        b2_bank = psum.tile([P, HIDDEN], F32, tag="y")
+        nc.tensor.matmul(
+            out=b2_bank[:],
+            lhsT=ones[:],
+            rhs=bias_rows[:, HIDDEN : 2 * HIDDEN],
+            start=True,
+            stop=True,
+        )
+        b1_cols = const.tile([P, HIDDEN], F32)
+        nc.vector.tensor_copy(
+            out=b1_cols[:].rearrange("q (j p) -> q j p", j=PACK),
+            in_=b1_bank[:].rearrange("q (p j) -> q j p", j=PACK),
+        )
+        b2_cols = const.tile([P, HIDDEN], F32)
+        nc.vector.tensor_copy(out=b2_cols[:], in_=b2_bank[:])
+
+        w1_grouped = const.tile([P, PASSES_1 * HIDDEN * PACK], BF16, align_bytes=64)
+        w1_codes = const.tile([P, PASSES_1, HIDDEN], U32, align_bytes=64)
+        w1_scales = const.tile([P, PASSES_1, HIDDEN], U8, align_bytes=64)
+        for g in range(PASSES_1):
+            for half in range(2):
+                bank = psum.tile([P, PACK, P], F32, tag=("xt", "zt")[g])
+                for a in range(2):
+                    words = w1_rows[:, 2 * half + a, :].bitcast(F32)
+                    for u in range(2):
+                        block = 2 * g + u
+                        nc.tensor.transpose(
+                            bank[:, 2 * a + u, :], words[:, block * P : (block + 1) * P], ident[:]
+                        )
+                first = (2 * g + half) * 2 * BANK_WORDS
+                interleave_out_of_psum(
+                    (nc.scalar.copy, nc.vector.tensor_copy)[half],
+                    w1_grouped[:, first : first + 2 * BANK_WORDS],
+                    bank,
+                )
+        for g in range(PASSES_1):
+            nc.vector.quantize_mx(
+                out=w1_codes[:, g, :].bitcast(FP8X4),
+                scales=w1_scales[:, g, :],
+                in_=w1_grouped[:, g * HIDDEN * PACK : (g + 1) * HIDDEN * PACK],
+            )
+
+        w2_grouped = const.tile([P, HIDDEN * PACK], BF16, align_bytes=64)
+        w2_codes = const.tile([P, HIDDEN], U32, align_bytes=64)
+        w2_scales = const.tile([P, HIDDEN], U8, align_bytes=64)
+
+        def prepare_w2():
+            for half in range(2):
+                bank = psum.tile([P, PACK, P], F32, tag="zt")
+                for a in range(2):
+                    words = w2_rows[:, 2 * half + a, :].bitcast(F32)
+                    for u in range(2):
+                        nc.tensor.transpose(
+                            bank[:, 2 * a + u, :],
+                            words.rearrange("o (q u) -> o u q", u=2)[:, u, :],
+                            ident[:],
+                        )
+                first = half * 2 * BANK_WORDS
+                interleave_out_of_psum(
+                    (nc.scalar.copy, nc.vector.tensor_copy)[half],
+                    w2_grouped[:, first : first + 2 * BANK_WORDS],
+                    bank,
+                )
+            nc.vector.quantize_mx(
+                out=w2_codes[:].bitcast(FP8X4), scales=w2_scales[:], in_=w2_grouped[:]
+            )
+
+        live = {}
+
+        def transpose_x(t):
+            words = x_chunks[t // CHUNK][:, t % CHUNK, :].bitcast(F32)
+            xt = psum.tile([P, PACK, P], F32, tag="xt")
+            for block in range(PACK):
+                nc.tensor.transpose(
+                    xt[:, block, :], words[:, block * P : (block + 1) * P], ident[:]
+                )
+            live["xt", t] = xt
+
+        def copy_x(t):
+            x_grouped = work.tile([P, K1], BF16, align_bytes=64)
+            copy = nc.vector.tensor_copy if t % 3 == 2 else nc.scalar.copy
+            interleave_out_of_psum(copy, x_grouped[:], live["xt", t])
+            live["x_grouped", t] = x_grouped
+
+        def quantise_x(t):
+            x_codes = work.tile([P, PASSES_1 * P], U32, align_bytes=64)
+            x_scales = work.tile([P, PASSES_1 * P], U8, align_bytes=64)
+            nc.vector.quantize_mx(
+                out=x_codes[:].bitcast(FP8X4), scales=x_scales[:], in_=live["x_grouped", t][:]
+            )
+            live["x_codes", t] = x_codes
+            live["x_scales", t] = x_scales
+
+        def matmul_1(t):
+            a = psum.tile([P, HIDDEN], F32, tag="a")
+            for g in range(PASSES_1):
+                rows = slice(g * P, (g + 1) * P)
+                nc.tensor.matmul_mx(
+                    out=a[:],
+                    lhsT=live["x_codes", t][:, rows].bitcast(FP8X4),
+                    lhsT_scale=live["x_scales", t][:, rows],
+                    rhs=w1_codes[:, g, :].bitcast(FP8X4),
+                    rhs_scale=w1_scales[:, g, :],
+                    start=(g == 0),
+                    stop=(g == PASSES_1 - 1),
+                )
+            live["a", t] = a
+
+        def add_bias_1(t):
+            z = work.tile([P, HIDDEN], F32)
+            nc.vector.tensor_tensor(out=z[:], in0=live["a", t][:], in1=b1_cols[:], op=ALU.add)
+            live["z", t] = z
+
+        def inverse_norm(t):
+            squares = work.tile([P, HIDDEN], BF16)
+            sum_squares = work.tile([P, 1], F32)
+            nc.scalar.activation(
+                out=squares[:], in_=live["z", t][:], func=ACT.Square, accum_out=sum_squares[:]
+            )
+            floored = work.tile([P, 1], F32)
+            nc.gpsimd.tensor_scalar_max(out=floored[:], in0=sum_squares[:], scalar1=EPS * EPS)
+            inv_norm = work.tile([P, 1], F32)
+            nc.gpsimd.tensor_tensor(
+                out=inv_norm[:], in0=floored[:], in1=minus_half[:], op=ALU.pow
+            )
+            live["inv_norm", t] = inv_norm
+
+        def scale_z(t):
+            z_unit = work.tile([P, HIDDEN], F32)
+            nc.vector.tensor_scalar_mul(
+                out=z_unit[:], in0=live["z", t][:], scalar1=live["inv_norm", t][:]
+            )
+            live["z_unit", t] = z_unit
+
+        def transpose_z(t):
+            zt = psum.tile([P, PACK, P], F32, tag="zt")
+            for j in range(PACK):
+                nc.tensor.transpose(
+                    zt[:, j, :], live["z_unit", t][:, j * P : (j + 1) * P], ident[:]
+                )
+            live["zt", t] = zt
+
+        def tanh_1(t):
+            t_grouped = work.tile([P, P, PACK], BF16, align_bytes=64)
+            nc.scalar.activation(
+                out=t_grouped[:], in_=live["zt", t][:].rearrange("p j b -> p b j"), func=ACT.Tanh
+            )
+            live["t_grouped", t] = t_grouped
+
+        def quantise_t(t):
+            t_codes = work.tile([P, P], U32, align_bytes=64)
+            t_scales = work.tile([P, P], U8, align_bytes=64)
+            nc.vector.quantize_mx(
+                out=t_codes[:].bitcast(FP8X4),
+                scales=t_scales[:],
+                in_=live["t_grouped", t][:].rearrange("p b j -> p (b j)"),
+            )
+            live["t_codes", t] = t_codes
+            live["t_scales", t] = t_scales
+
+        def matmul_2(t):
+            y = psum.tile([P, HIDDEN], F32, tag="y")
+            nc.tensor.matmul_mx(
+                out=y[:],
+                lhsT=live["t_codes", t][:].bitcast(FP8X4),
+                lhsT_scale=live["t_scales", t][:],
+                rhs=w2_codes[:].bitcast(FP8X4),
+                rhs_scale=w2_scales[:],
+                start=True,
+                stop=True,
+            )
+            live["y", t] = y
+
+        def add_bias_2(t):
+            y_biased = work.tile([P, HIDDEN], F32)
+            nc.vector.tensor_tensor(
+                out=y_biased[:], in0=live["y", t][:], in1=b2_cols[:], op=ALU.add
+            )
+            live["y_biased", t] = y_biased
+
+        def tanh_2_and_store(t):
+            result = work.tile([P, HIDDEN], F32)
+            nc.scalar.activation(out=result[:], in_=live["y_biased", t][:], func=ACT.Tanh)
+            nc.sync.dma_start(out=out_rows[:, t, :], in_=result[:])
+
+        def run(stage, t):
+            if 0 <= t < TILES:
+                stage(t)
+
+        def pipeline_step(s):
+            run(transpose_x, s)
+            run(transpose_z, s - LAG_TRANSPOSE_Z)
+            run(matmul_1, s - LAG_MATMUL_1)
+            run(matmul_2, s - LAG_MATMUL_2)
+            run(copy_x, s - LAG_COPY_X)
+            run(tanh_1, s - LAG_TANH_1)
+            run(add_bias_1, s - LAG_BIAS_1)
+            run(add_bias_2, s - LAG_OUT)
+            run(inverse_norm, s - LAG_BIAS_1)
+            run(tanh_2_and_store, s - LAG_OUT)
+            run(scale_z, s - LAG_SCALE)
+            run(quantise_x, s - LAG_COPY_X)
+            run(quantise_t, s - LAG_TANH_1)
+
+        for s in range(LAG_TRANSPOSE_Z):
+            pipeline_step(s)
+        prepare_w2()
+        for s in range(LAG_TRANSPOSE_Z, STEPS):
+            pipeline_step(s)

@@ -25,14 +25,18 @@ BANK_WORDS = 512
 FLOPS = 2 * BATCH * K1 * HIDDEN + 2 * BATCH * HIDDEN * HIDDEN
 
 LAG_COPY_X = 1
-LAG_MATMUL_1 = 2
-LAG_BIAS_1 = 3
-LAG_SCALE = 4
-LAG_TRANSPOSE_Z = 5
-LAG_TANH_1 = 6
-LAG_MATMUL_2 = 7
-LAG_OUT = 8
-STEPS = TILES + LAG_OUT
+LAG_QUANTISE_X = 2
+LAG_MATMUL_1 = 3
+LAG_BIAS_1 = 4
+LAG_NORM = 5
+LAG_SCALE = 7
+LAG_TRANSPOSE_Z = 8
+LAG_TANH_1 = 9
+LAG_QUANTISE_T = 10
+LAG_MATMUL_2 = 11
+LAG_BIAS_2 = 12
+LAG_TANH_2 = 13
+STEPS = TILES + LAG_TANH_2
 
 
 def tile_modelgraphpolicy_pa_t_kernel(
@@ -45,21 +49,23 @@ def tile_modelgraphpolicy_pa_t_kernel(
 
     with ExitStack() as stack:
         const = stack.enter_context(tc.tile_pool(name="const", bufs=1))
-        work = stack.enter_context(tc.tile_pool(name="work", bufs=4))
+        work = stack.enter_context(tc.tile_pool(name="work", bufs=6))
         psum = stack.enter_context(tc.psum_pool(name="psum", bufs=2))
         stack.enter_context(tc.manual_schedule())
 
         bias_rows = const.tile([P, 2 * HIDDEN], BF16)
         nc.vector.memset(bias_rows[:], 0.0)
-        nc.scalar.dma_start(
-            out=bias_rows[0:1, 0:HIDDEN], in_=up_b1.rearrange("(o h) -> o h", o=1)
-        )
-        nc.scalar.dma_start(
-            out=bias_rows[0:1, HIDDEN : 2 * HIDDEN], in_=up_b2.rearrange("(o h) -> o h", o=1)
-        )
 
         w1_rows = const.tile([P, PACK, K1], BF16)
-        nc.sync.dma_start(out=w1_rows[:], in_=up_w1.rearrange("(p j) k -> p j k", j=PACK))
+        w1_view = up_w1.rearrange("(p j) k -> p j k", j=PACK)
+        nc.sync.dma_start(out=w1_rows[:, :, 0:K_PASS], in_=w1_view[:, :, 0:K_PASS])
+        nc.sync.dma_start(
+            out=bias_rows[0:1, 0:HIDDEN], in_=up_b1.rearrange("(o h) -> o h", o=1)
+        )
+        nc.sync.dma_start(
+            out=bias_rows[0:1, HIDDEN : 2 * HIDDEN], in_=up_b2.rearrange("(o h) -> o h", o=1)
+        )
+        nc.sync.dma_start(out=w1_rows[:, :, K_PASS:K1], in_=w1_view[:, :, K_PASS:K1])
         w2_rows = const.tile([P, PACK, HIDDEN], BF16)
 
         x_chunks = []
@@ -90,42 +96,45 @@ def tile_modelgraphpolicy_pa_t_kernel(
 
         def interleave_out_of_psum(copy, grouped, bank):
             copy(
-                out=grouped.bitcast(F32).rearrange("q (a n u) -> q a n u", a=2, u=2),
-                in_=bank[:].rearrange("q (a u) n -> q a n u", u=2),
+                out=grouped.bitcast(F32).rearrange("q (i n u) -> q i n u", i=2, u=2),
+                in_=bank[:].rearrange("q (i u) n -> q i n u", u=2),
             )
 
-        b1_bank = psum.tile([P, HIDDEN], F32, tag="a")
-        nc.tensor.matmul(
-            out=b1_bank[:], lhsT=ones[:], rhs=bias_rows[:, 0:HIDDEN], start=True, stop=True
-        )
-        b2_bank = psum.tile([P, HIDDEN], F32, tag="y")
-        nc.tensor.matmul(
-            out=b2_bank[:],
-            lhsT=ones[:],
-            rhs=bias_rows[:, HIDDEN : 2 * HIDDEN],
-            start=True,
-            stop=True,
-        )
         b1_cols = const.tile([P, HIDDEN], F32)
-        nc.vector.tensor_copy(
-            out=b1_cols[:].rearrange("q (j p) -> q j p", j=PACK),
-            in_=b1_bank[:].rearrange("q (p j) -> q j p", j=PACK),
-        )
         b2_cols = const.tile([P, HIDDEN], F32)
-        nc.vector.tensor_copy(out=b2_cols[:], in_=b2_bank[:])
+
+        def spread_biases():
+            b1_bank = psum.tile([P, HIDDEN], F32, tag="a")
+            nc.tensor.matmul(
+                out=b1_bank[:], lhsT=ones[:], rhs=bias_rows[:, 0:HIDDEN], start=True, stop=True
+            )
+            b2_bank = psum.tile([P, HIDDEN], F32, tag="y")
+            nc.tensor.matmul(
+                out=b2_bank[:],
+                lhsT=ones[:],
+                rhs=bias_rows[:, HIDDEN : 2 * HIDDEN],
+                start=True,
+                stop=True,
+            )
+            nc.vector.tensor_copy(
+                out=b1_cols[:].rearrange("q (j p) -> q j p", j=PACK),
+                in_=b1_bank[:].rearrange("q (p j) -> q j p", j=PACK),
+            )
+            nc.scalar.copy(out=b2_cols[:], in_=b2_bank[:])
 
         w1_grouped = const.tile([P, PASSES_1 * HIDDEN * PACK], BF16, align_bytes=64)
         w1_codes = const.tile([P, PASSES_1, HIDDEN], U32, align_bytes=64)
         w1_scales = const.tile([P, PASSES_1, HIDDEN], U8, align_bytes=64)
-        for g in range(PASSES_1):
+
+        def transpose_w1(g):
             for half in range(2):
                 bank = psum.tile([P, PACK, P], F32, tag=("xt", "zt")[g])
-                for a in range(2):
-                    words = w1_rows[:, 2 * half + a, :].bitcast(F32)
+                for i in range(2):
+                    words = w1_rows[:, 2 * half + i, :].bitcast(F32)
                     for u in range(2):
                         block = 2 * g + u
                         nc.tensor.transpose(
-                            bank[:, 2 * a + u, :], words[:, block * P : (block + 1) * P], ident[:]
+                            bank[:, 2 * i + u, :], words[:, block * P : (block + 1) * P], ident[:]
                         )
                 first = (2 * g + half) * 2 * BANK_WORDS
                 interleave_out_of_psum(
@@ -133,7 +142,8 @@ def tile_modelgraphpolicy_pa_t_kernel(
                     w1_grouped[:, first : first + 2 * BANK_WORDS],
                     bank,
                 )
-        for g in range(PASSES_1):
+
+        def quantise_w1(g):
             nc.vector.quantize_mx(
                 out=w1_codes[:, g, :].bitcast(FP8X4),
                 scales=w1_scales[:, g, :],
@@ -147,11 +157,11 @@ def tile_modelgraphpolicy_pa_t_kernel(
         def prepare_w2():
             for half in range(2):
                 bank = psum.tile([P, PACK, P], F32, tag="zt")
-                for a in range(2):
-                    words = w2_rows[:, 2 * half + a, :].bitcast(F32)
+                for i in range(2):
+                    words = w2_rows[:, 2 * half + i, :].bitcast(F32)
                     for u in range(2):
                         nc.tensor.transpose(
-                            bank[:, 2 * a + u, :],
+                            bank[:, 2 * i + u, :],
                             words.rearrange("o (q u) -> o u q", u=2)[:, u, :],
                             ident[:],
                         )
@@ -295,13 +305,18 @@ def tile_modelgraphpolicy_pa_t_kernel(
             run(copy_x, s - LAG_COPY_X)
             run(tanh_1, s - LAG_TANH_1)
             run(add_bias_1, s - LAG_BIAS_1)
-            run(add_bias_2, s - LAG_OUT)
-            run(inverse_norm, s - LAG_BIAS_1)
-            run(tanh_2_and_store, s - LAG_OUT)
+            run(add_bias_2, s - LAG_BIAS_2)
+            run(inverse_norm, s - LAG_NORM)
+            run(tanh_2_and_store, s - LAG_TANH_2)
             run(scale_z, s - LAG_SCALE)
-            run(quantise_x, s - LAG_COPY_X)
-            run(quantise_t, s - LAG_TANH_1)
+            run(quantise_x, s - LAG_QUANTISE_X)
+            run(quantise_t, s - LAG_QUANTISE_T)
 
+        transpose_w1(0)
+        spread_biases()
+        transpose_w1(1)
+        quantise_w1(0)
+        quantise_w1(1)
         for s in range(LAG_TRANSPOSE_Z):
             pipeline_step(s)
         prepare_w2()

@@ -29,9 +29,9 @@ LAG_QUANTISE_X = 2
 LAG_MATMUL_1 = 3
 LAG_BIAS_1 = 4
 LAG_NORM = 5
-LAG_SCALE = 7
-LAG_TRANSPOSE_Z = 8
-LAG_TANH_1 = 9
+LAG_TANH_1 = 7
+LAG_TRANSPOSE_T = 8
+LAG_COPY_T = 9
 LAG_QUANTISE_T = 10
 LAG_MATMUL_2 = 11
 LAG_BIAS_2 = 12
@@ -117,8 +117,8 @@ def tile_modelgraphpolicy_pa_t_kernel(
                 stop=True,
             )
             nc.vector.tensor_copy(
-                out=b1_cols[:].rearrange("q (j p) -> q j p", j=PACK),
-                in_=b1_bank[:].rearrange("q (p j) -> q j p", j=PACK),
+                out=b1_cols[:].rearrange("q (u p e) -> q u p e", u=2, e=2),
+                in_=b1_bank[:].rearrange("q (p u e) -> q u p e", u=2, e=2),
             )
             nc.scalar.copy(out=b2_cols[:], in_=b2_bank[:])
 
@@ -137,10 +137,11 @@ def tile_modelgraphpolicy_pa_t_kernel(
                             bank[:, 2 * i + u, :], words[:, block * P : (block + 1) * P], ident[:]
                         )
                 first = (2 * g + half) * 2 * BANK_WORDS
-                interleave_out_of_psum(
-                    (nc.scalar.copy, nc.vector.tensor_copy)[half],
-                    w1_grouped[:, first : first + 2 * BANK_WORDS],
-                    bank,
+                (nc.scalar.copy, nc.vector.tensor_copy)[half](
+                    out=w1_grouped[:, first : first + 2 * BANK_WORDS]
+                    .bitcast(F32)
+                    .rearrange("q (p i u) -> q p i u", i=2, u=2),
+                    in_=bank[:].rearrange("q (i u) p -> q p i u", u=2),
                 )
 
         def quantise_w1(g):
@@ -235,25 +236,25 @@ def tile_modelgraphpolicy_pa_t_kernel(
             )
             live["inv_norm", t] = inv_norm
 
-        def scale_z(t):
-            z_unit = work.tile([P, HIDDEN], F32)
-            nc.vector.tensor_scalar_mul(
-                out=z_unit[:], in0=live["z", t][:], scalar1=live["inv_norm", t][:]
-            )
-            live["z_unit", t] = z_unit
-
-        def transpose_z(t):
-            zt = psum.tile([P, PACK, P], F32, tag="zt")
-            for j in range(PACK):
-                nc.tensor.transpose(
-                    zt[:, j, :], live["z_unit", t][:, j * P : (j + 1) * P], ident[:]
-                )
-            live["zt", t] = zt
-
         def tanh_1(t):
-            t_grouped = work.tile([P, P, PACK], BF16, align_bytes=64)
+            t_rows = work.tile([P, HIDDEN], BF16)
             nc.scalar.activation(
-                out=t_grouped[:], in_=live["zt", t][:].rearrange("p j b -> p b j"), func=ACT.Tanh
+                out=t_rows[:], in_=live["z", t][:], func=ACT.Tanh, scale=live["inv_norm", t][:]
+            )
+            live["t_rows", t] = t_rows
+
+        def transpose_t(t):
+            words = live["t_rows", t][:].bitcast(F32)
+            tt = psum.tile([P, 2, P], F32, tag="zt")
+            for u in range(2):
+                nc.tensor.transpose(tt[:, u, :], words[:, u * P : (u + 1) * P], ident[:])
+            live["tt", t] = tt
+
+        def copy_t(t):
+            t_grouped = work.tile([P, P * PACK], BF16, align_bytes=64)
+            nc.vector.tensor_copy(
+                out=t_grouped[:].bitcast(F32).rearrange("q (b u) -> q b u", u=2),
+                in_=live["tt", t][:].rearrange("q u b -> q b u"),
             )
             live["t_grouped", t] = t_grouped
 
@@ -263,7 +264,7 @@ def tile_modelgraphpolicy_pa_t_kernel(
             nc.vector.quantize_mx(
                 out=t_codes[:].bitcast(FP8X4),
                 scales=t_scales[:],
-                in_=live["t_grouped", t][:].rearrange("p b j -> p (b j)"),
+                in_=live["t_grouped", t][:],
             )
             live["t_codes", t] = t_codes
             live["t_scales", t] = t_scales
@@ -299,16 +300,16 @@ def tile_modelgraphpolicy_pa_t_kernel(
 
         def pipeline_step(s):
             run(transpose_x, s)
-            run(transpose_z, s - LAG_TRANSPOSE_Z)
+            run(transpose_t, s - LAG_TRANSPOSE_T)
             run(matmul_1, s - LAG_MATMUL_1)
             run(matmul_2, s - LAG_MATMUL_2)
             run(copy_x, s - LAG_COPY_X)
-            run(tanh_1, s - LAG_TANH_1)
+            run(copy_t, s - LAG_COPY_T)
             run(add_bias_1, s - LAG_BIAS_1)
             run(add_bias_2, s - LAG_BIAS_2)
             run(inverse_norm, s - LAG_NORM)
+            run(tanh_1, s - LAG_TANH_1)
             run(tanh_2_and_store, s - LAG_TANH_2)
-            run(scale_z, s - LAG_SCALE)
             run(quantise_x, s - LAG_QUANTISE_X)
             run(quantise_t, s - LAG_QUANTISE_T)
 
@@ -317,8 +318,8 @@ def tile_modelgraphpolicy_pa_t_kernel(
         transpose_w1(1)
         quantise_w1(0)
         quantise_w1(1)
-        for s in range(LAG_TRANSPOSE_Z):
+        for s in range(LAG_TRANSPOSE_T):
             pipeline_step(s)
         prepare_w2()
-        for s in range(LAG_TRANSPOSE_Z, STEPS):
+        for s in range(LAG_TRANSPOSE_T, STEPS):
             pipeline_step(s)

@@ -30,12 +30,12 @@ LAG_MATMUL_1 = 3
 LAG_BIAS_1 = 4
 LAG_NORM = 5
 LAG_TANH_1 = 7
-LAG_TRANSPOSE_T = 8
-LAG_COPY_T = 9
-LAG_QUANTISE_T = 10
-LAG_MATMUL_2 = 11
-LAG_BIAS_2 = 12
-LAG_TANH_2 = 13
+LAG_TRANSPOSE_T = 10
+LAG_COPY_T = 11
+LAG_QUANTISE_T = 11
+LAG_MATMUL_2 = 12
+LAG_BIAS_2 = 13
+LAG_TANH_2 = 14
 STEPS = TILES + LAG_TANH_2
 
 
@@ -58,29 +58,34 @@ def tile_modelgraphpolicy_pa_t_kernel(
 
         w1_rows = const.tile([P, PACK, K1], BF16)
         w1_view = up_w1.rearrange("(p j) k -> p j k", j=PACK)
-        nc.sync.dma_start(out=w1_rows[:, :, 0:K_PASS], in_=w1_view[:, :, 0:K_PASS])
+        x_rows = {}
+
+        def load_x(first, count):
+            x = const.tile([P, count, K1], BF16, name="x%d" % first)
+            tiles = slice(first, first + count)
+            nc.sync.dma_start(out=x[:, :, 0:STATE], in_=state_rows[:, tiles, :])
+            nc.sync.dma_start(out=x[:, :, STATE:K1], in_=action_rows[:, tiles, :])
+            for i in range(count):
+                x_rows[first + i] = x[:, i, :]
+
+        nc.sync.dma_start(out=w1_rows[:, 0:2, :], in_=w1_view[:, 0:2, :])
+        nc.sync.dma_start(out=w1_rows[:, 2:4, :], in_=w1_view[:, 2:4, :])
         nc.sync.dma_start(
             out=bias_rows[0:1, 0:HIDDEN], in_=up_b1.rearrange("(o h) -> o h", o=1)
         )
         nc.sync.dma_start(
             out=bias_rows[0:1, HIDDEN : 2 * HIDDEN], in_=up_b2.rearrange("(o h) -> o h", o=1)
         )
-        nc.sync.dma_start(out=w1_rows[:, :, K_PASS:K1], in_=w1_view[:, :, K_PASS:K1])
+        load_x(0, 1)
+        load_x(1, 1)
         w2_rows = const.tile([P, PACK, HIDDEN], BF16)
 
-        x_chunks = []
-
-        def load_x(c):
-            x = const.tile([P, CHUNK, K1], BF16, name="x%d" % c)
-            tiles = slice(c * CHUNK, (c + 1) * CHUNK)
-            nc.sync.dma_start(out=x[:, :, 0:STATE], in_=state_rows[:, tiles, :])
-            nc.sync.dma_start(out=x[:, :, STATE:K1], in_=action_rows[:, tiles, :])
-            x_chunks.append(x)
-
-        load_x(0)
-        nc.sync.dma_start(out=w2_rows[:], in_=up_w2_self.rearrange("(c p) k -> p c k", p=P))
         for c in range(1, TILES // CHUNK):
-            load_x(c)
+            load_x(c * CHUNK, CHUNK)
+            if c == 2:
+                nc.sync.dma_start(
+                    out=w2_rows[:], in_=up_w2_self.rearrange("(c p) k -> p c k", p=P)
+                )
 
         zero_col = const.tile([P, 1], F32)
         nc.vector.memset(zero_col[:], 0.0)
@@ -103,11 +108,17 @@ def tile_modelgraphpolicy_pa_t_kernel(
         b1_cols = const.tile([P, HIDDEN], F32)
         b2_cols = const.tile([P, HIDDEN], F32)
 
-        def spread_biases():
+        def spread_bias_1():
             b1_bank = psum.tile([P, HIDDEN], F32, tag="a")
             nc.tensor.matmul(
                 out=b1_bank[:], lhsT=ones[:], rhs=bias_rows[:, 0:HIDDEN], start=True, stop=True
             )
+            nc.scalar.copy(
+                out=b1_cols[:].rearrange("q (u p e) -> q u p e", u=2, e=2),
+                in_=b1_bank[:].rearrange("q (p u e) -> q u p e", u=2, e=2),
+            )
+
+        def spread_bias_2():
             b2_bank = psum.tile([P, HIDDEN], F32, tag="y")
             nc.tensor.matmul(
                 out=b2_bank[:],
@@ -116,19 +127,17 @@ def tile_modelgraphpolicy_pa_t_kernel(
                 start=True,
                 stop=True,
             )
-            nc.vector.tensor_copy(
-                out=b1_cols[:].rearrange("q (u p e) -> q u p e", u=2, e=2),
-                in_=b1_bank[:].rearrange("q (p u e) -> q u p e", u=2, e=2),
-            )
             nc.scalar.copy(out=b2_cols[:], in_=b2_bank[:])
 
         w1_grouped = const.tile([P, PASSES_1 * HIDDEN * PACK], BF16, align_bytes=64)
         w1_codes = const.tile([P, PASSES_1, HIDDEN], U32, align_bytes=64)
         w1_scales = const.tile([P, PASSES_1, HIDDEN], U8, align_bytes=64)
 
-        def transpose_w1(g):
-            for half in range(2):
-                bank = psum.tile([P, PACK, P], F32, tag=("xt", "zt")[g])
+        w1_banks = {}
+
+        def transpose_w1(half):
+            for g in range(PASSES_1):
+                bank = psum.tile([P, PACK, P], F32, tag=("zt", "y")[half], name="w1_bank")
                 for i in range(2):
                     words = w1_rows[:, 2 * half + i, :].bitcast(F32)
                     for u in range(2):
@@ -136,28 +145,37 @@ def tile_modelgraphpolicy_pa_t_kernel(
                         nc.tensor.transpose(
                             bank[:, 2 * i + u, :], words[:, block * P : (block + 1) * P], ident[:]
                         )
+                w1_banks[g, half] = bank
+
+        def copy_w1(half):
+            for g in range(PASSES_1):
                 first = (2 * g + half) * 2 * BANK_WORDS
-                (nc.scalar.copy, nc.vector.tensor_copy)[half](
+                (nc.scalar.copy, nc.vector.tensor_copy)[g](
                     out=w1_grouped[:, first : first + 2 * BANK_WORDS]
                     .bitcast(F32)
                     .rearrange("q (p i u) -> q p i u", i=2, u=2),
-                    in_=bank[:].rearrange("q (i u) p -> q p i u", u=2),
+                    in_=w1_banks[g, half][:].rearrange("q (i u) p -> q p i u", u=2),
                 )
 
-        def quantise_w1(g):
-            nc.vector.quantize_mx(
-                out=w1_codes[:, g, :].bitcast(FP8X4),
-                scales=w1_scales[:, g, :],
-                in_=w1_grouped[:, g * HIDDEN * PACK : (g + 1) * HIDDEN * PACK],
-            )
+        def quantise_w1(half):
+            columns = slice(half * HIDDEN // 2, (half + 1) * HIDDEN // 2)
+            for g in range(PASSES_1):
+                first = (2 * g + half) * 2 * BANK_WORDS
+                nc.vector.quantize_mx(
+                    out=w1_codes[:, g, columns].bitcast(FP8X4),
+                    scales=w1_scales[:, g, columns],
+                    in_=w1_grouped[:, first : first + 2 * BANK_WORDS],
+                )
 
         w2_grouped = const.tile([P, HIDDEN * PACK], BF16, align_bytes=64)
         w2_codes = const.tile([P, HIDDEN], U32, align_bytes=64)
         w2_scales = const.tile([P, HIDDEN], U8, align_bytes=64)
 
-        def prepare_w2():
+        w2_banks = {}
+
+        def transpose_w2():
             for half in range(2):
-                bank = psum.tile([P, PACK, P], F32, tag="zt")
+                bank = psum.tile([P, PACK, P], F32, tag="zt", name="w2_bank")
                 for i in range(2):
                     words = w2_rows[:, 2 * half + i, :].bitcast(F32)
                     for u in range(2):
@@ -166,12 +184,15 @@ def tile_modelgraphpolicy_pa_t_kernel(
                             words.rearrange("o (q u) -> o u q", u=2)[:, u, :],
                             ident[:],
                         )
-                first = half * 2 * BANK_WORDS
-                interleave_out_of_psum(
-                    (nc.scalar.copy, nc.vector.tensor_copy)[half],
-                    w2_grouped[:, first : first + 2 * BANK_WORDS],
-                    bank,
-                )
+                w2_banks[half] = bank
+
+        def copy_w2(half):
+            first = half * 2 * BANK_WORDS
+            interleave_out_of_psum(
+                nc.vector.tensor_copy, w2_grouped[:, first : first + 2 * BANK_WORDS], w2_banks[half]
+            )
+
+        def quantise_w2():
             nc.vector.quantize_mx(
                 out=w2_codes[:].bitcast(FP8X4), scales=w2_scales[:], in_=w2_grouped[:]
             )
@@ -179,7 +200,7 @@ def tile_modelgraphpolicy_pa_t_kernel(
         live = {}
 
         def transpose_x(t):
-            words = x_chunks[t // CHUNK][:, t % CHUNK, :].bitcast(F32)
+            words = x_rows[t].bitcast(F32)
             xt = psum.tile([P, PACK, P], F32, tag="xt")
             for block in range(PACK):
                 nc.tensor.transpose(
@@ -189,7 +210,7 @@ def tile_modelgraphpolicy_pa_t_kernel(
 
         def copy_x(t):
             x_grouped = work.tile([P, K1], BF16, align_bytes=64)
-            copy = nc.vector.tensor_copy if t % 3 == 2 else nc.scalar.copy
+            copy = nc.vector.tensor_copy if t % 3 == 0 else nc.scalar.copy
             interleave_out_of_psum(copy, x_grouped[:], live["xt", t])
             live["x_grouped", t] = x_grouped
 
@@ -301,25 +322,36 @@ def tile_modelgraphpolicy_pa_t_kernel(
         def pipeline_step(s):
             run(transpose_x, s)
             run(transpose_t, s - LAG_TRANSPOSE_T)
-            run(matmul_1, s - LAG_MATMUL_1)
             run(matmul_2, s - LAG_MATMUL_2)
+            run(matmul_1, s - LAG_MATMUL_1)
             run(copy_x, s - LAG_COPY_X)
-            run(copy_t, s - LAG_COPY_T)
-            run(add_bias_1, s - LAG_BIAS_1)
-            run(add_bias_2, s - LAG_BIAS_2)
+            run(tanh_2_and_store, s - LAG_TANH_2)
             run(inverse_norm, s - LAG_NORM)
             run(tanh_1, s - LAG_TANH_1)
-            run(tanh_2_and_store, s - LAG_TANH_2)
             run(quantise_x, s - LAG_QUANTISE_X)
+            run(copy_t, s - LAG_COPY_T)
+            run(add_bias_2, s - LAG_BIAS_2)
+            run(add_bias_1, s - LAG_BIAS_1)
             run(quantise_t, s - LAG_QUANTISE_T)
 
         transpose_w1(0)
-        spread_biases()
+        copy_w1(0)
         transpose_w1(1)
         quantise_w1(0)
+        copy_w1(1)
+        spread_bias_1()
+        pipeline_step(0)
         quantise_w1(1)
-        for s in range(LAG_TRANSPOSE_T):
+        pipeline_step(1)
+        pipeline_step(2)
+        for s in range(3, STEPS):
             pipeline_step(s)
-        prepare_w2()
-        for s in range(LAG_TRANSPOSE_T, STEPS):
-            pipeline_step(s)
+            if s == 8:
+                transpose_w2()
+            if s == 9:
+                copy_w2(0)
+                spread_bias_2()
+            if s == 10:
+                copy_w2(1)
+            if s == 11:
+                quantise_w2()

@@ -19,6 +19,7 @@ K1 = STATE + ACTION
 PASSES_1 = K1 // K_PASS
 TILES = BATCH // P
 CHUNK = 2
+WARM_MATMULS = 6
 EPS = 1e-12
 BANK_WORDS = 512
 
@@ -53,6 +54,13 @@ def tile_modelgraphpolicy_pa_t_kernel(
         psum = stack.enter_context(tc.psum_pool(name="psum", bufs=2))
         stack.enter_context(tc.manual_schedule())
 
+        ones = const.tile([P, P], BF16)
+        nc.vector.memset(ones[:], 1.0)
+        zeros = const.tile([P, HIDDEN], BF16)
+        nc.vector.memset(zeros[:], 0.0)
+        unused = psum.tile([P, HIDDEN], F32, tag="xt")
+        for i in range(WARM_MATMULS):
+            nc.tensor.matmul(out=unused[:], lhsT=ones[:], rhs=zeros[:], start=True, stop=True)
         bias_rows = const.tile([P, 2 * HIDDEN], BF16)
         nc.vector.memset(bias_rows[:], 0.0)
 
@@ -82,7 +90,7 @@ def tile_modelgraphpolicy_pa_t_kernel(
 
         for c in range(1, TILES // CHUNK):
             load_x(c * CHUNK, CHUNK)
-            if c == 2:
+            if c == 3:
                 nc.sync.dma_start(
                     out=w2_rows[:], in_=up_w2_self.rearrange("(c p) k -> p c k", p=P)
                 )
@@ -92,8 +100,6 @@ def tile_modelgraphpolicy_pa_t_kernel(
         table_warm = const.tile([P, 1], F32)
         nc.scalar.activation(out=table_warm[:], in_=zero_col[:], func=ACT.Tanh)
 
-        ones = const.tile([P, P], BF16)
-        nc.vector.memset(ones[:], 1.0)
         minus_half = const.tile([P, 1], F32)
         nc.vector.memset(minus_half[:], -0.5)
         ident = const.tile([P, P], F32)
@@ -303,17 +309,29 @@ def tile_modelgraphpolicy_pa_t_kernel(
             )
             live["y", t] = y
 
+        def pieces(t):
+            count = 2 if t == TILES - 1 else 1
+            width = HIDDEN // count
+            return [slice(i * width, (i + 1) * width) for i in range(count)]
+
         def add_bias_2(t):
             y_biased = work.tile([P, HIDDEN], F32)
-            nc.vector.tensor_tensor(
-                out=y_biased[:], in0=live["y", t][:], in1=b2_cols[:], op=ALU.add
-            )
+            for piece in pieces(t):
+                nc.vector.tensor_tensor(
+                    out=y_biased[:, piece],
+                    in0=live["y", t][:, piece],
+                    in1=b2_cols[:, piece],
+                    op=ALU.add,
+                )
             live["y_biased", t] = y_biased
 
         def tanh_2_and_store(t):
             result = work.tile([P, HIDDEN], F32)
-            nc.scalar.activation(out=result[:], in_=live["y_biased", t][:], func=ACT.Tanh)
-            nc.sync.dma_start(out=out_rows[:, t, :], in_=result[:])
+            for piece in pieces(t):
+                nc.scalar.activation(
+                    out=result[:, piece], in_=live["y_biased", t][:, piece], func=ACT.Tanh
+                )
+                nc.sync.dma_start(out=out_rows[:, t, piece], in_=result[:, piece])
 
         def run(stage, t):
             if 0 <= t < TILES:

@@ -19,7 +19,7 @@ K1 = STATE + ACTION
 PASSES_1 = K1 // K_PASS
 TILES = BATCH // P
 CHUNK = 2
-WARM_MATMULS = 6
+WARM_MATMULS = 4
 EPS = 1e-12
 BANK_WORDS = 512
 
@@ -326,7 +326,7 @@ def tile_modelgraphpolicy_pa_t_kernel(
             live["y_biased", t] = y_biased
 
         def tanh_2_and_store(t):
-            result = work.tile([P, HIDDEN], F32)
+            result = const.tile([P, HIDDEN], F32, name="result%d" % t)
             for piece in pieces(t):
                 nc.scalar.activation(
                     out=result[:, piece], in_=live["y_biased", t][:, piece], func=ACT.Tanh

from contextlib import ExitStack

import concourse.mybir as mybir
from concourse.masks import make_identity

F32 = mybir.dt.float32
BF16 = mybir.dt.bfloat16
U32 = mybir.dt.uint32
U8 = mybir.dt.uint8
FP8X4 = mybir.dt.float8_e4m3fn_x4
ACT = mybir.ActivationFunctionType
ALU = mybir.AluOpType

P = 128
PACK = 4
K_PASS = P * PACK
BATCH, STATE, ACTION, HIDDEN = 4096, 896, 128, 512
K1 = STATE + ACTION
PASSES_1 = K1 // K_PASS
TILES = BATCH // P
CHUNK = 2
WARM_MATMULS = 4
EPS = 1e-12
BANK_WORDS = 512

FLOPS = 2 * BATCH * K1 * HIDDEN + 2 * BATCH * HIDDEN * HIDDEN

LAG_COPY_X = 1
LAG_QUANTISE_X = 2
LAG_MATMUL_1 = 3
LAG_BIAS_1 = 4
LAG_NORM = 5
LAG_TANH_1 = 7
LAG_TRANSPOSE_T = 10
LAG_COPY_T = 11
LAG_QUANTISE_T = 11
LAG_MATMUL_2 = 12
LAG_BIAS_2 = 13
LAG_TANH_2 = 14
STEPS = TILES + LAG_TANH_2


def tile_modelgraphpolicy_pa_t_kernel(
    tc, state, action, up_w1, up_b1, up_w2_self, up_b2, out
):
    nc = tc.nc
    state_rows = state.rearrange("(p t) d -> p t d", t=TILES)
    action_rows = action.rearrange("(p t) d -> p t d", t=TILES)
    out_rows = out.rearrange("(p t) d -> p t d", t=TILES)

    with ExitStack() as stack:
        const = stack.enter_context(tc.tile_pool(name="const", bufs=1))
        work = stack.enter_context(tc.tile_pool(name="work", bufs=6))
        psum = stack.enter_context(tc.psum_pool(name="psum", bufs=2))
        stack.enter_context(tc.manual_schedule())

        ones = const.tile([P, P], BF16)
        nc.vector.memset(ones[:], 1.0)
        zeros = const.tile([P, HIDDEN], BF16)
        nc.vector.memset(zeros[:], 0.0)
        unused = psum.tile([P, HIDDEN], F32, tag="xt")
        for i in range(WARM_MATMULS):
            nc.tensor.matmul(out=unused[:], lhsT=ones[:], rhs=zeros[:], start=True, stop=True)
        bias_rows = const.tile([P, 2 * HIDDEN], BF16)
        nc.vector.memset(bias_rows[:], 0.0)

        w1_rows = const.tile([P, PACK, K1], BF16)
        w1_view = up_w1.rearrange("(p j) k -> p j k", j=PACK)
        x_rows = {}

        def load_x(first, count):
            x = const.tile([P, count, K1], BF16, name="x%d" % first)
            tiles = slice(first, first + count)
            nc.sync.dma_start(out=x[:, :, 0:STATE], in_=state_rows[:, tiles, :])
            nc.sync.dma_start(out=x[:, :, STATE:K1], in_=action_rows[:, tiles, :])
            for i in range(count):
                x_rows[first + i] = x[:, i, :]

        nc.sync.dma_start(out=w1_rows[:, 0:2, :], in_=w1_view[:, 0:2, :])
        nc.sync.dma_start(out=w1_rows[:, 2:4, :], in_=w1_view[:, 2:4, :])
        nc.sync.dma_start(
            out=bias_rows[0:1, 0:HIDDEN], in_=up_b1.rearrange("(o h) -> o h", o=1)
        )
        nc.sync.dma_start(
            out=bias_rows[0:1, HIDDEN : 2 * HIDDEN], in_=up_b2.rearrange("(o h) -> o h", o=1)
        )
        load_x(0, 1)
        load_x(1, 1)
        w2_rows = const.tile([P, PACK, HIDDEN], BF16)

        for c in range(1, TILES // CHUNK):
            load_x(c * CHUNK, CHUNK)
            if c == 3:
                nc.sync.dma_start(
                    out=w2_rows[:], in_=up_w2_self.rearrange("(c p) k -> p c k", p=P)
                )

        zero_col = const.tile([P, 1], F32)
        nc.vector.memset(zero_col[:], 0.0)
        table_warm = const.tile([P, 1], F32)
        nc.scalar.activation(out=table_warm[:], in_=zero_col[:], func=ACT.Tanh)

        minus_half = const.tile([P, 1], F32)
        nc.vector.memset(minus_half[:], -0.5)
        ident = const.tile([P, P], F32)
        make_identity(nc, ident[:])

        def interleave_out_of_psum(copy, grouped, bank):
            copy(
                out=grouped.bitcast(F32).rearrange("q (i n u) -> q i n u", i=2, u=2),
                in_=bank[:].rearrange("q (i u) n -> q i n u", u=2),
            )

        b1_cols = const.tile([P, HIDDEN], F32)
        b2_cols = const.tile([P, HIDDEN], F32)

        def spread_bias_1():
            b1_bank = psum.tile([P, HIDDEN], F32, tag="a")
            nc.tensor.matmul(
                out=b1_bank[:], lhsT=ones[:], rhs=bias_rows[:, 0:HIDDEN], start=True, stop=True
            )
            nc.scalar.copy(
                out=b1_cols[:].rearrange("q (u p e) -> q u p e", u=2, e=2),
                in_=b1_bank[:].rearrange("q (p u e) -> q u p e", u=2, e=2),
            )

        def spread_bias_2():
            b2_bank = psum.tile([P, HIDDEN], F32, tag="y")
            nc.tensor.matmul(
                out=b2_bank[:],
                lhsT=ones[:],
                rhs=bias_rows[:, HIDDEN : 2 * HIDDEN],
                start=True,
                stop=True,
            )
            nc.scalar.copy(out=b2_cols[:], in_=b2_bank[:])

        w1_grouped = const.tile([P, PASSES_1 * HIDDEN * PACK], BF16, align_bytes=64)
        w1_codes = const.tile([P, PASSES_1, HIDDEN], U32, align_bytes=64)
        w1_scales = const.tile([P, PASSES_1, HIDDEN], U8, align_bytes=64)

        w1_banks = {}

        def transpose_w1(half):
            for g in range(PASSES_1):
                bank = psum.tile([P, PACK, P], F32, tag=("zt", "y")[half], name="w1_bank")
                for i in range(2):
                    words = w1_rows[:, 2 * half + i, :].bitcast(F32)
                    for u in range(2):
                        block = 2 * g + u
                        nc.tensor.transpose(
                            bank[:, 2 * i + u, :], words[:, block * P : (block + 1) * P], ident[:]
                        )
                w1_banks[g, half] = bank

        def copy_w1(half):
            for g in range(PASSES_1):
                first = (2 * g + half) * 2 * BANK_WORDS
                (nc.scalar.copy, nc.vector.tensor_copy)[g](
                    out=w1_grouped[:, first : first + 2 * BANK_WORDS]
                    .bitcast(F32)
                    .rearrange("q (p i u) -> q p i u", i=2, u=2),
                    in_=w1_banks[g, half][:].rearrange("q (i u) p -> q p i u", u=2),
                )

        def quantise_w1(half):
            columns = slice(half * HIDDEN // 2, (half + 1) * HIDDEN // 2)
            for g in range(PASSES_1):
                first = (2 * g + half) * 2 * BANK_WORDS
                nc.vector.quantize_mx(
                    out=w1_codes[:, g, columns].bitcast(FP8X4),
                    scales=w1_scales[:, g, columns],
                    in_=w1_grouped[:, first : first + 2 * BANK_WORDS],
                )

        w2_grouped = const.tile([P, HIDDEN * PACK], BF16, align_bytes=64)
        w2_codes = const.tile([P, HIDDEN], U32, align_bytes=64)
        w2_scales = const.tile([P, HIDDEN], U8, align_bytes=64)

        w2_banks = {}

        def transpose_w2():
            for half in range(2):
                bank = psum.tile([P, PACK, P], F32, tag="zt", name="w2_bank")
                for i in range(2):
                    words = w2_rows[:, 2 * half + i, :].bitcast(F32)
                    for u in range(2):
                        nc.tensor.transpose(
                            bank[:, 2 * i + u, :],
                            words.rearrange("o (q u) -> o u q", u=2)[:, u, :],
                            ident[:],
                        )
                w2_banks[half] = bank

        def copy_w2(half):
            first = half * 2 * BANK_WORDS
            interleave_out_of_psum(
                nc.vector.tensor_copy, w2_grouped[:, first : first + 2 * BANK_WORDS], w2_banks[half]
            )

        def quantise_w2():
            nc.vector.quantize_mx(
                out=w2_codes[:].bitcast(FP8X4), scales=w2_scales[:], in_=w2_grouped[:]
            )

        live = {}

        def transpose_x(t):
            words = x_rows[t].bitcast(F32)
            xt = psum.tile([P, PACK, P], F32, tag="xt")
            for block in range(PACK):
                nc.tensor.transpose(
                    xt[:, block, :], words[:, block * P : (block + 1) * P], ident[:]
                )
            live["xt", t] = xt

        def copy_x(t):
            x_grouped = work.tile([P, K1], BF16, align_bytes=64)
            copy = nc.vector.tensor_copy if t % 3 == 0 else nc.scalar.copy
            interleave_out_of_psum(copy, x_grouped[:], live["xt", t])
            live["x_grouped", t] = x_grouped

        def quantise_x(t):
            x_codes = work.tile([P, PASSES_1 * P], U32, align_bytes=64)
            x_scales = work.tile([P, PASSES_1 * P], U8, align_bytes=64)
            nc.vector.quantize_mx(
                out=x_codes[:].bitcast(FP8X4), scales=x_scales[:], in_=live["x_grouped", t][:]
            )
            live["x_codes", t] = x_codes
            live["x_scales", t] = x_scales

        def matmul_1(t):
            a = psum.tile([P, HIDDEN], F32, tag="a")
            for g in range(PASSES_1):
                rows = slice(g * P, (g + 1) * P)
                nc.tensor.matmul_mx(
                    out=a[:],
                    lhsT=live["x_codes", t][:, rows].bitcast(FP8X4),
                    lhsT_scale=live["x_scales", t][:, rows],
                    rhs=w1_codes[:, g, :].bitcast(FP8X4),
                    rhs_scale=w1_scales[:, g, :],
                    start=(g == 0),
                    stop=(g == PASSES_1 - 1),
                )
            live["a", t] = a

        def add_bias_1(t):
            z = work.tile([P, HIDDEN], F32)
            nc.vector.tensor_tensor(out=z[:], in0=live["a", t][:], in1=b1_cols[:], op=ALU.add)
            live["z", t] = z

        def inverse_norm(t):
            squares = work.tile([P, HIDDEN], BF16)
            sum_squares = work.tile([P, 1], F32)
            nc.scalar.activation(
                out=squares[:], in_=live["z", t][:], func=ACT.Square, accum_out=sum_squares[:]
            )
            floored = work.tile([P, 1], F32)
            nc.gpsimd.tensor_scalar_max(out=floored[:], in0=sum_squares[:], scalar1=EPS * EPS)
            inv_norm = work.tile([P, 1], F32)
            nc.gpsimd.tensor_tensor(
                out=inv_norm[:], in0=floored[:], in1=minus_half[:], op=ALU.pow
            )
            live["inv_norm", t] = inv_norm

        def tanh_1(t):
            t_rows = work.tile([P, HIDDEN], BF16)
            nc.scalar.activation(
                out=t_rows[:], in_=live["z", t][:], func=ACT.Tanh, scale=live["inv_norm", t][:]
            )
            live["t_rows", t] = t_rows

        def transpose_t(t):
            words = live["t_rows", t][:].bitcast(F32)
            tt = psum.tile([P, 2, P], F32, tag="zt")
            for u in range(2):
                nc.tensor.transpose(tt[:, u, :], words[:, u * P : (u + 1) * P], ident[:])
            live["tt", t] = tt

        def copy_t(t):
            t_grouped = work.tile([P, P * PACK], BF16, align_bytes=64)
            nc.vector.tensor_copy(
                out=t_grouped[:].bitcast(F32).rearrange("q (b u) -> q b u", u=2),
                in_=live["tt", t][:].rearrange("q u b -> q b u"),
            )
            live["t_grouped", t] = t_grouped

        def quantise_t(t):
            t_codes = work.tile([P, P], U32, align_bytes=64)
            t_scales = work.tile([P, P], U8, align_bytes=64)
            nc.vector.quantize_mx(
                out=t_codes[:].bitcast(FP8X4),
                scales=t_scales[:],
                in_=live["t_grouped", t][:],
            )
            live["t_codes", t] = t_codes
            live["t_scales", t] = t_scales

        def matmul_2(t):
            y = psum.tile([P, HIDDEN], F32, tag="y")
            nc.tensor.matmul_mx(
                out=y[:],
                lhsT=live["t_codes", t][:].bitcast(FP8X4),
                lhsT_scale=live["t_scales", t][:],
                rhs=w2_codes[:].bitcast(FP8X4),
                rhs_scale=w2_scales[:],
                start=True,
                stop=True,
            )
            live["y", t] = y

        def pieces(t):
            count = 2 if t == TILES - 1 else 1
            width = HIDDEN // count
            return [slice(i * width, (i + 1) * width) for i in range(count)]

        def add_bias_2(t):
            y_biased = work.tile([P, HIDDEN], F32)
            for piece in pieces(t):
                nc.vector.tensor_tensor(
                    out=y_biased[:, piece],
                    in0=live["y", t][:, piece],
                    in1=b2_cols[:, piece],
                    op=ALU.add,
                )
            live["y_biased", t] = y_biased

        def tanh_2_and_store(t):
            result = const.tile([P, HIDDEN], F32, name="result%d" % t)
            for piece in pieces(t):
                nc.scalar.activation(
                    out=result[:, piece], in_=live["y_biased", t][:, piece], func=ACT.Tanh
                )
                nc.sync.dma_start(out=out_rows[:, t, piece], in_=result[:, piece])

        def run(stage, t):
            if 0 <= t < TILES:
                stage(t)

        def pipeline_step(s):
            run(transpose_x, s)
            run(transpose_t, s - LAG_TRANSPOSE_T)
            run(matmul_2, s - LAG_MATMUL_2)
            run(matmul_1, s - LAG_MATMUL_1)
            run(copy_x, s - LAG_COPY_X)
            run(tanh_2_and_store, s - LAG_TANH_2)
            run(inverse_norm, s - LAG_NORM)
            run(tanh_1, s - LAG_TANH_1)
            run(quantise_x, s - LAG_QUANTISE_X)
            run(copy_t, s - LAG_COPY_T)
            run(add_bias_2, s - LAG_BIAS_2)
            run(add_bias_1, s - LAG_BIAS_1)
            run(quantise_t, s - LAG_QUANTISE_T)

        transpose_w1(0)
        copy_w1(0)
        transpose_w1(1)
        quantise_w1(0)
        copy_w1(1)
        spread_bias_1()
        pipeline_step(0)
        quantise_w1(1)
        pipeline_step(1)
        pipeline_step(2)
        for s in range(3, STEPS):
            pipeline_step(s)
            if s == 8:
                transpose_w2()
            if s == 9:
                copy_w2(0)
                spread_bias_2()
            if s == 10:
                copy_w2(1)
            if s == 11:
                quantise_w2()
